import numpy as np
import ml_dtypes


def mxq(x, axis, fmt="e4m3"):
    dtype, down = {"e4m3": (ml_dtypes.float8_e4m3fn, 7), "e5m2": (ml_dtypes.float8_e5m2, 14)}[fmt]
    v = np.moveaxis(np.asarray(x, np.float32).astype(ml_dtypes.bfloat16).astype(np.float64), axis, -1)
    blocks = v.reshape(v.shape[:-1] + (-1, 32))
    amax = np.abs(blocks).max(-1, keepdims=True)
    byte = np.maximum(np.where(amax > 0, np.frexp(amax)[1] - 1 + 127, 0) - down, 1)
    scale = np.exp2(byte - 127.0)
    codes = (blocks / scale).astype(np.float32).astype(dtype).astype(np.float64)
    return np.moveaxis((codes * scale).reshape(v.shape), -1, axis)


WIDE = False


def mx_kscale(k):
    if not WIDE:
        return np.ones(k)
    levels = np.array([10, -10, 5, -5, 0])
    a = np.random.permutation(np.resize(levels, k // 512 * 4)).reshape(k // 512, 4)
    idx = np.arange(k)
    return np.exp2(a[idx // 512, idx % 128 // 32])


BF16 = ml_dtypes.bfloat16


def bf(x):
    return np.asarray(x, np.float32).astype(BF16)


def f64(x):
    return np.asarray(x).astype(np.float64)


B, N, D, H, DH = 1, 512, 512, 16, 32
INNER = H * DH
S = 2 * DH


def dpfp(u):
    u2 = np.concatenate([np.maximum(u, 0.0), np.maximum(-u, 0.0)], axis=-1)
    return u2 * np.roll(u2, 1, axis=-1)


def setup_inputs():
    s, t = mx_kscale(D), mx_kscale(N)
    f = dpfp(np.random.standard_normal((B, H, N, DH)))
    return {"x": bf(np.random.standard_normal((B, N, D)) * s),
            "wv": bf(np.random.standard_normal((D, INNER)) / np.sqrt(D) / s[:, None]),
            "beta": bf(np.random.standard_normal((B, H, N)) * t),
            "vo": bf(np.random.standard_normal((B, H, N, DH)) * 0.3),
            "k_phi": bf(f / f.sum(-1, keepdims=True) / t[:, None]),
            "W": bf(np.random.standard_normal((B, H, S, DH)))}


def reference(x, wv, beta, vo, k_phi, W):
    v = mxq(f64(x), 2, "e4m3") @ mxq(f64(wv), 0, "e4m3")
    v = v.reshape(B, N, H, DH).transpose(0, 2, 1, 3)
    dv = f64(beta)[..., None] * (v - f64(vo))
    return f64(W) + (mxq(f64(k_phi).transpose(0, 1, 3, 2), 3, "e4m3") @ mxq(dv, 2, "e4m3"))

@@ -1,0 +1,250 @@
+import concourse.mybir as mybir
+from concourse.masks import make_identity
+
+F32 = mybir.dt.float32
+BF16 = mybir.dt.bfloat16
+U32 = mybir.dt.uint32
+U8 = mybir.dt.uint8
+FP8X4 = mybir.dt.float8_e4m3fn_x4
+ALU = mybir.AluOpType
+
+P = 128
+PACK = 4
+TOKENS = 512
+MODEL = 512
+HEADS = 16
+HEAD_DIM = 32
+FEATURES = 64
+BANK = 512
+
+GROUPS = 4
+GROUP_HEADS = HEADS // GROUPS
+GROUP_COLS = GROUP_HEADS * HEAD_DIM
+PAIR = 2
+PAIRS = HEADS // PAIR
+PAIRS_PER_BANK = 4
+RUN = 4
+
+FLOPS = 2 * TOKENS * MODEL * HEADS * HEAD_DIM + 2 * HEADS * FEATURES * TOKENS * HEAD_DIM
+
+assert TOKENS == P * PACK and MODEL == P * PACK and PAIR * FEATURES == P
+
+
+def quantise(nc, grouped, codes, scales):
+    nc.vector.quantize_mx(out=codes.bitcast(FP8X4), scales=scales, in_=grouped)
+
+
+def tile_dpfpattention_pb_s_kernel(tc, x, wv, beta, vo, k_phi, W, out):
+    nc = tc.nc
+
+    x_rows = x.flatten_outer_dims().rearrange("(p j) k -> p (j k)", j=PACK)
+    vo_rows = vo.flatten_outer_dims().rearrange("(h p j) d -> p h (j d)", h=HEADS, j=PACK)
+    key_rows = k_phi.flatten_outer_dims().rearrange("(h p j) s -> p h (j s)", h=HEADS, j=PACK)
+    wv_rows = wv.rearrange("(u q e) c -> q u (e c)", u=2, e=2)
+    w_rows = W.flatten_outer_dims().rearrange("(a g s) d -> (g s) a d", a=PAIRS, g=PAIR)
+    out_rows = out.flatten_outer_dims().rearrange("(a g s) d -> (g s) a d", a=PAIRS, g=PAIR)
+
+    with tc.tile_pool(name="keep", bufs=1) as keep, tc.tile_pool(
+        name="diffs", bufs=2
+    ) as diffs, tc.psum_pool(name="flips", bufs=2) as flips, tc.psum_pool(
+        name="values", bufs=GROUPS
+    ) as values, tc.psum_pool(name="updates", bufs=PAIRS // PAIRS_PER_BANK) as updates, tc.manual_schedule():
+        identity = keep.tile([P, P], F32)
+        x_sb = keep.tile([P, PACK * MODEL], BF16)
+        x_grouped = keep.tile([P, TOKENS * PACK], BF16, align_bytes=64)
+        x_codes = keep.tile([P, TOKENS], U32, align_bytes=64)
+        x_scales = keep.tile([P, TOKENS], U8, align_bytes=64)
+        wv_sb = keep.tile([P, PACK, HEADS * HEAD_DIM], BF16)
+        wv_grouped = keep.tile([P, HEADS * HEAD_DIM, PACK], BF16, align_bytes=64)
+        wv_codes = keep.tile([P, HEADS * HEAD_DIM], U32, align_bytes=64)
+        wv_scales = keep.tile([P, HEADS * HEAD_DIM], U8, align_bytes=64)
+        beta_rows = keep.tile([P, TOKENS], BF16)
+        beta_sb = keep.tile([P, HEADS * PACK], BF16)
+        vo_sb = keep.tile([P, HEADS, PACK * HEAD_DIM], BF16)
+        key_sb = keep.tile([P, HEADS, PACK * FEATURES], BF16)
+        key_grouped = keep.tile([P, HEADS, FEATURES, PACK], BF16, align_bytes=64)
+        key_codes = keep.tile([P, HEADS * FEATURES], U32, align_bytes=64)
+        key_scales = keep.tile([P, HEADS * FEATURES], U8, align_bytes=64)
+        dv_grouped = keep.tile([P, HEADS, HEAD_DIM, PACK], BF16, align_bytes=64)
+        dv_codes = keep.tile([P, HEADS * HEAD_DIM], U32, align_bytes=64)
+        dv_scales = keep.tile([P, HEADS * HEAD_DIM], U8, align_bytes=64)
+        w_sb = keep.tile([P, PAIRS, HEAD_DIM], BF16)
+        result = keep.tile([P, PAIRS, HEAD_DIM], F32)
+
+        make_identity(nc, identity[:])
+        nc.vector.memset(beta_rows[:], 0.0)
+
+        half_row = PACK * MODEL // 2
+        for half in range(2):
+            cols = slice(half * half_row, (half + 1) * half_row)
+            nc.sync.dma_start(out=x_sb[:, cols], in_=x_rows[:, cols])
+        nc.sync.dma_start(out=beta_rows[0:HEADS, :], in_=beta.flatten_outer_dims())
+        nc.sync.dma_start(out=wv_sb[:].rearrange("q (u e) c -> q u (e c)", u=2), in_=wv_rows)
+        for group in range(GROUPS):
+            heads = slice(group * GROUP_HEADS, (group + 1) * GROUP_HEADS)
+            nc.sync.dma_start(out=vo_sb[:, heads, :], in_=vo_rows[:, heads, :])
+            nc.sync.dma_start(out=key_sb[:, heads, :], in_=key_rows[:, heads, :])
+        nc.sync.dma_start(out=w_sb[:], in_=w_rows)
+
+        x_words = x_sb[:].bitcast(F32)
+        x_grouped_words = x_grouped[:].bitcast(F32)
+        for half in range(2):
+            flipped = flips.tile([P, BANK], F32)
+            for piece in range(BANK // P):
+                nc.tensor.transpose(
+                    flipped[:, piece * P : (piece + 1) * P],
+                    x_words[:, half * BANK + piece * P : half * BANK + (piece + 1) * P],
+                    identity[:],
+                )
+            nc.scalar.copy(
+                out=x_grouped_words[:, half * BANK : (half + 1) * BANK].rearrange(
+                    "q (j p u) -> q j p u", j=2, u=2
+                ),
+                in_=flipped[:].rearrange("q (j u p) -> q j p u", j=2, u=2),
+            )
+
+        beta_words = beta_rows[:].bitcast(F32).rearrange("h (p w) -> h w p", w=2)
+        beta_flipped = flips.tile([P, BANK], F32, tag="flipped")
+        for w in range(2):
+            nc.tensor.transpose(beta_flipped[:, w * P : (w + 1) * P], beta_words[:, w, :], identity[:])
+        nc.scalar.copy(
+            out=beta_sb[:].bitcast(F32).rearrange("p (h w) -> p h w", w=2),
+            in_=beta_flipped[:, 0 : 2 * P].rearrange("p (w h) -> p h w", w=2)[:, 0:HEADS, :],
+        )
+
+        def regroup_wv(engine_copy, group):
+            cols = slice(group * GROUP_COLS, (group + 1) * GROUP_COLS)
+            engine_copy(
+                out=wv_grouped[:, cols, :].rearrange("q (c i) t -> q c t i", i=RUN),
+                in_=wv_sb[:, :, cols].rearrange("q t (c i) -> q c t i", i=RUN),
+            )
+
+        def quantise_x(half):
+            quantise(
+                nc,
+                x_grouped[:, half * half_row : (half + 1) * half_row],
+                x_codes[:, half * 2 * P : (half + 1) * 2 * P],
+                x_scales[:, half * 2 * P : (half + 1) * 2 * P],
+            )
+
+        quantise_x(0)
+        regroup_wv(nc.vector.tensor_copy, 0)
+        regroup_wv(nc.scalar.copy, 2)
+        quantise_x(1)
+        regroup_wv(nc.vector.tensor_copy, 1)
+        regroup_wv(nc.scalar.copy, 3)
+        for group in range(GROUPS):
+            cols = slice(group * GROUP_COLS, (group + 1) * GROUP_COLS)
+            quantise(
+                nc,
+                wv_grouped[:, cols, :].rearrange("q c t -> q (c t)"),
+                wv_codes[:, cols],
+                wv_scales[:, cols],
+            )
+
+        v_banks = []
+        for group in range(GROUPS):
+            cols = slice(group * GROUP_COLS, (group + 1) * GROUP_COLS)
+            v_bank = values.tile([P, BANK], F32)
+            v_banks.append(v_bank)
+            for j in range(PACK):
+                tokens = slice(j * P, (j + 1) * P)
+                nc.tensor.matmul_mx(
+                    out=v_bank[:, j * GROUP_COLS : (j + 1) * GROUP_COLS],
+                    lhsT=x_codes[:, tokens].bitcast(FP8X4),
+                    lhsT_scale=x_scales[:, tokens],
+                    rhs=wv_codes[:, cols].bitcast(FP8X4),
+                    rhs_scale=wv_scales[:, cols],
+                    start=True,
+                    stop=True,
+                )
+
+        def subtract(group):
+            heads = slice(group * GROUP_HEADS, (group + 1) * GROUP_HEADS)
+            diff = diffs.tile([P, GROUP_HEADS, HEAD_DIM, PACK], F32)
+            nc.vector.tensor_tensor(
+                out=diff[:],
+                in0=v_banks[group][:].rearrange("p (j h d) -> p h d j", j=PACK, h=GROUP_HEADS),
+                in1=vo_sb[:, heads, :].rearrange("p h (j d) -> p h d j", j=PACK),
+                op=ALU.subtract,
+            )
+            return diff
+
+        def scale(group, diff):
+            heads = slice(group * GROUP_HEADS, (group + 1) * GROUP_HEADS)
+            strengths = beta_sb[:, group * GROUP_HEADS * PACK : (group + 1) * GROUP_HEADS * PACK]
+            nc.vector.tensor_tensor(
+                out=dv_grouped[:, heads, :, :],
+                in0=diff[:],
+                in1=strengths.rearrange("p (h j) -> p h j", j=PACK)
+                .unsqueeze(2)
+                .to_broadcast([P, GROUP_HEADS, HEAD_DIM, PACK]),
+                op=ALU.mult,
+            )
+
+        def regroup_keys(group):
+            for head in range(group * GROUP_HEADS, (group + 1) * GROUP_HEADS):
+                nc.scalar.copy(
+                    out=key_grouped[:, head, :, :].rearrange("p (s i) j -> p s j i", i=RUN),
+                    in_=key_sb[:, head, :].rearrange("p (j s i) -> p s j i", j=PACK, i=RUN),
+                )
+
+        def quantise_group(group):
+            heads = slice(group * GROUP_HEADS, (group + 1) * GROUP_HEADS)
+            key_cols = slice(group * GROUP_HEADS * FEATURES, (group + 1) * GROUP_HEADS * FEATURES)
+            dv_cols = slice(group * GROUP_COLS, (group + 1) * GROUP_COLS)
+            quantise(
+                nc,
+                key_grouped[:, heads, :, :].rearrange("p h s j -> p (h s j)"),
+                key_codes[:, key_cols],
+                key_scales[:, key_cols],
+            )
+            quantise(
+                nc,
+                dv_grouped[:, heads, :, :].rearrange("p h d j -> p (h d j)"),
+                dv_codes[:, dv_cols],
+                dv_scales[:, dv_cols],
+            )
+
+        def second_matmul(pair, update_bank):
+            key_cols = slice(pair * P, (pair + 1) * P)
+            dv_cols = slice(pair * PAIR * HEAD_DIM, (pair + 1) * PAIR * HEAD_DIM)
+            place = (pair % PAIRS_PER_BANK) * PAIR * HEAD_DIM
+            nc.tensor.matmul_mx(
+                out=update_bank[:, place : place + PAIR * HEAD_DIM],
+                lhsT=key_codes[:, key_cols].bitcast(FP8X4),
+                lhsT_scale=key_scales[:, key_cols],
+                rhs=dv_codes[:, dv_cols].bitcast(FP8X4),
+                rhs_scale=dv_scales[:, dv_cols],
+                start=True,
+                stop=True,
+            )
+
+        update_banks = []
+        diff_now = subtract(0)
+        for group in range(GROUPS):
+            diff_next = subtract(group + 1) if group + 1 < GROUPS else None
+            scale(group, diff_now)
+            diff_now = diff_next
+            regroup_keys(group)
+            quantise_group(group)
+            for pair in range(group * GROUP_HEADS // PAIR, (group + 1) * GROUP_HEADS // PAIR):
+                if pair % PAIRS_PER_BANK == 0:
+                    update_bank = updates.tile([P, BANK], F32)
+                    update_banks.append(update_bank)
+                second_matmul(pair, update_banks[-1])
+
+        for bank in range(PAIRS // PAIRS_PER_BANK):
+            pairs = slice(bank * PAIRS_PER_BANK, (bank + 1) * PAIRS_PER_BANK)
+            used = PAIRS_PER_BANK * PAIR * HEAD_DIM
+            for g in range(PAIR):
+                rows = slice(g * FEATURES, (g + 1) * FEATURES)
+                nc.vector.tensor_tensor(
+                    out=result[rows, pairs, :],
+                    in0=update_banks[bank][rows, 0:used].rearrange(
+                        "r (a g d) -> r a g d", a=PAIRS_PER_BANK, g=PAIR
+                    )[:, :, g, :],
+                    in1=w_sb[rows, pairs, :],
+                    op=ALU.add,
+                )
+            nc.sync.dma_start(out=out_rows[:, pairs, :], in_=result[:, pairs, :])

@@ -16,12 +16,14 @@ HEADS = 16
 HEAD_DIM = 32
 FEATURES = 64
 BANK = 512
+PSUM_BANKS = 8
 
 GROUPS = 4
 GROUP_HEADS = HEADS // GROUPS
 GROUP_COLS = GROUP_HEADS * HEAD_DIM
 PAIR = 2
 PAIRS = HEADS // PAIR
+GROUP_PAIRS = GROUP_HEADS // PAIR
 PAIRS_PER_BANK = 4
 RUN = 4
 
@@ -46,9 +48,9 @@ def tile_dpfpattention_pb_s_kernel(tc, x, wv, beta, vo, k_phi, W, out):
 
     with tc.tile_pool(name="keep", bufs=1) as keep, tc.tile_pool(
         name="diffs", bufs=2
-    ) as diffs, tc.psum_pool(name="flips", bufs=2) as flips, tc.psum_pool(
-        name="values", bufs=GROUPS
-    ) as values, tc.psum_pool(name="updates", bufs=PAIRS // PAIRS_PER_BANK) as updates, tc.manual_schedule():
+    ) as diffs, tc.psum_pool(name="values", bufs=GROUPS) as values, tc.psum_pool(
+        name="others", bufs=PSUM_BANKS - GROUPS
+    ) as others, tc.manual_schedule():
         identity = keep.tile([P, P], F32)
         x_sb = keep.tile([P, PACK * MODEL], BF16)
         x_grouped = keep.tile([P, TOKENS * PACK], BF16, align_bytes=64)
@@ -80,71 +82,60 @@ def tile_dpfpattention_pb_s_kernel(tc, x, wv, beta, vo, k_phi, W, out):
             nc.sync.dma_start(out=x_sb[:, cols], in_=x_rows[:, cols])
         nc.sync.dma_start(out=beta_rows[0:HEADS, :], in_=beta.flatten_outer_dims())
         nc.sync.dma_start(out=wv_sb[:].rearrange("q (u e) c -> q u (e c)", u=2), in_=wv_rows)
-        for group in range(GROUPS):
+        def load_vo(group):
             heads = slice(group * GROUP_HEADS, (group + 1) * GROUP_HEADS)
             nc.sync.dma_start(out=vo_sb[:, heads, :], in_=vo_rows[:, heads, :])
-            nc.sync.dma_start(out=key_sb[:, heads, :], in_=key_rows[:, heads, :])
+
+        load_vo(0)
+        for group in range(GROUPS):
+            if group + 1 < GROUPS:
+                load_vo(group + 1)
+            for pair in range(group * GROUP_PAIRS, (group + 1) * GROUP_PAIRS):
+                heads = slice(pair * PAIR, (pair + 1) * PAIR)
+                nc.sync.dma_start(out=key_sb[:, heads, :], in_=key_rows[:, heads, :])
         nc.sync.dma_start(out=w_sb[:], in_=w_rows)
 
         x_words = x_sb[:].bitcast(F32)
         x_grouped_words = x_grouped[:].bitcast(F32)
-        for half in range(2):
-            flipped = flips.tile([P, BANK], F32)
-            for piece in range(BANK // P):
-                nc.tensor.transpose(
-                    flipped[:, piece * P : (piece + 1) * P],
-                    x_words[:, half * BANK + piece * P : half * BANK + (piece + 1) * P],
-                    identity[:],
-                )
-            nc.scalar.copy(
-                out=x_grouped_words[:, half * BANK : (half + 1) * BANK].rearrange(
-                    "q (j p u) -> q j p u", j=2, u=2
-                ),
-                in_=flipped[:].rearrange("q (j u p) -> q j p u", j=2, u=2),
+        def quantise_x(j):
+            tokens = slice(j * P, (j + 1) * P)
+            quantise(nc, x_grouped[:, j * P * PACK : (j + 1) * P * PACK], x_codes[:, tokens], x_scales[:, tokens])
+
+        for j in range(PACK):
+            flipped = others.tile([P, 2 * P], F32, tag="other")
+            for u in range(2):
+                word = (2 * j + u) * P
+                nc.tensor.transpose(flipped[:, u * P : (u + 1) * P], x_words[:, word : word + P], identity[:])
+            copy_out = nc.scalar.copy if j % 2 == 0 else nc.vector.tensor_copy
+            copy_out(
+                out=x_grouped_words[:, j * 2 * P : (j + 1) * 2 * P].rearrange("q (p u) -> q p u", u=2),
+                in_=flipped[:].rearrange("q (u p) -> q p u", u=2),
             )
+            if j > 0:
+                quantise_x(j - 1)
 
         beta_words = beta_rows[:].bitcast(F32).rearrange("h (p w) -> h w p", w=2)
-        beta_flipped = flips.tile([P, BANK], F32, tag="flipped")
+        beta_flipped = others.tile([P, 2 * P], F32, tag="other")
         for w in range(2):
             nc.tensor.transpose(beta_flipped[:, w * P : (w + 1) * P], beta_words[:, w, :], identity[:])
         nc.scalar.copy(
             out=beta_sb[:].bitcast(F32).rearrange("p (h w) -> p h w", w=2),
-            in_=beta_flipped[:, 0 : 2 * P].rearrange("p (w h) -> p h w", w=2)[:, 0:HEADS, :],
+            in_=beta_flipped[:].rearrange("p (w h) -> p h w", w=2)[:, 0:HEADS, :],
         )
 
-        def regroup_wv(engine_copy, group):
+        def regroup_wv(group):
             cols = slice(group * GROUP_COLS, (group + 1) * GROUP_COLS)
-            engine_copy(
+            regroup = nc.vector.tensor_copy if group % 2 == 0 else nc.scalar.copy
+            regroup(
                 out=wv_grouped[:, cols, :].rearrange("q (c i) t -> q c t i", i=RUN),
                 in_=wv_sb[:, :, cols].rearrange("q t (c i) -> q c t i", i=RUN),
             )
 
-        def quantise_x(half):
-            quantise(
-                nc,
-                x_grouped[:, half * half_row : (half + 1) * half_row],
-                x_codes[:, half * 2 * P : (half + 1) * 2 * P],
-                x_scales[:, half * 2 * P : (half + 1) * 2 * P],
-            )
-
-        quantise_x(0)
-        regroup_wv(nc.vector.tensor_copy, 0)
-        regroup_wv(nc.scalar.copy, 2)
-        quantise_x(1)
-        regroup_wv(nc.vector.tensor_copy, 1)
-        regroup_wv(nc.scalar.copy, 3)
-        for group in range(GROUPS):
-            cols = slice(group * GROUP_COLS, (group + 1) * GROUP_COLS)
-            quantise(
-                nc,
-                wv_grouped[:, cols, :].rearrange("q c t -> q (c t)"),
-                wv_codes[:, cols],
-                wv_scales[:, cols],
-            )
-
         v_banks = []
-        for group in range(GROUPS):
+
+        def first_matmul(group):
             cols = slice(group * GROUP_COLS, (group + 1) * GROUP_COLS)
+            quantise(nc, wv_grouped[:, cols, :].rearrange("q c t -> q (c t)"), wv_codes[:, cols], wv_scales[:, cols])
             v_bank = values.tile([P, BANK], F32)
             v_banks.append(v_bank)
             for j in range(PACK):
@@ -158,6 +149,15 @@ def tile_dpfpattention_pb_s_kernel(tc, x, wv, beta, vo, k_phi, W, out):
                     start=True,
                     stop=True,
                 )
+
+        regroup_wv(0)
+        regroup_wv(1)
+        quantise_x(PACK - 1)
+        first_matmul(0)
+        regroup_wv(2)
+        regroup_wv(3)
+        for group in range(1, GROUPS):
+            first_matmul(group)
 
         def subtract(group):
             heads = slice(group * GROUP_HEADS, (group + 1) * GROUP_HEADS)
@@ -182,23 +182,24 @@ def tile_dpfpattention_pb_s_kernel(tc, x, wv, beta, vo, k_phi, W, out):
                 op=ALU.mult,
             )
 
-        def regroup_keys(group):
-            for head in range(group * GROUP_HEADS, (group + 1) * GROUP_HEADS):
+        def quantise_keys(pair):
+            heads = slice(pair * PAIR, (pair + 1) * PAIR)
+            key_cols = slice(pair * P, (pair + 1) * P)
+            for head in range(pair * PAIR, (pair + 1) * PAIR):
                 nc.scalar.copy(
                     out=key_grouped[:, head, :, :].rearrange("p (s i) j -> p s j i", i=RUN),
                     in_=key_sb[:, head, :].rearrange("p (j s i) -> p s j i", j=PACK, i=RUN),
                 )
-
-        def quantise_group(group):
-            heads = slice(group * GROUP_HEADS, (group + 1) * GROUP_HEADS)
-            key_cols = slice(group * GROUP_HEADS * FEATURES, (group + 1) * GROUP_HEADS * FEATURES)
-            dv_cols = slice(group * GROUP_COLS, (group + 1) * GROUP_COLS)
             quantise(
                 nc,
                 key_grouped[:, heads, :, :].rearrange("p h s j -> p (h s j)"),
                 key_codes[:, key_cols],
                 key_scales[:, key_cols],
             )
+
+        def quantise_dv(group):
+            heads = slice(group * GROUP_HEADS, (group + 1) * GROUP_HEADS)
+            dv_cols = slice(group * GROUP_COLS, (group + 1) * GROUP_COLS)
             quantise(
                 nc,
                 dv_grouped[:, heads, :, :].rearrange("p h d j -> p (h d j)"),
@@ -226,22 +227,23 @@ def tile_dpfpattention_pb_s_kernel(tc, x, wv, beta, vo, k_phi, W, out):
             diff_next = subtract(group + 1) if group + 1 < GROUPS else None
             scale(group, diff_now)
             diff_now = diff_next
-            regroup_keys(group)
-            quantise_group(group)
-            for pair in range(group * GROUP_HEADS // PAIR, (group + 1) * GROUP_HEADS // PAIR):
+            quantise_keys(group * GROUP_PAIRS)
+            quantise_dv(group)
+            for pair in range(group * GROUP_PAIRS + 1, (group + 1) * GROUP_PAIRS):
+                quantise_keys(pair)
+            for pair in range(group * GROUP_PAIRS, (group + 1) * GROUP_PAIRS):
                 if pair % PAIRS_PER_BANK == 0:
-                    update_bank = updates.tile([P, BANK], F32)
+                    update_bank = others.tile([P, PAIRS_PER_BANK * PAIR * HEAD_DIM], F32, tag="other")
                     update_banks.append(update_bank)
                 second_matmul(pair, update_banks[-1])
 
         for bank in range(PAIRS // PAIRS_PER_BANK):
             pairs = slice(bank * PAIRS_PER_BANK, (bank + 1) * PAIRS_PER_BANK)
-            used = PAIRS_PER_BANK * PAIR * HEAD_DIM
             for g in range(PAIR):
                 rows = slice(g * FEATURES, (g + 1) * FEATURES)
                 nc.vector.tensor_tensor(
                     out=result[rows, pairs, :],
-                    in0=update_banks[bank][rows, 0:used].rearrange(
+                    in0=update_banks[bank][rows, :].rearrange(
                         "r (a g d) -> r a g d", a=PAIRS_PER_BANK, g=PAIR
                     )[:, :, g, :],
                     in1=w_sb[rows, pairs, :],

@@ -23,7 +23,6 @@ GROUP_HEADS = HEADS // GROUPS
 GROUP_COLS = GROUP_HEADS * HEAD_DIM
 PAIR = 2
 PAIRS = HEADS // PAIR
-GROUP_PAIRS = GROUP_HEADS // PAIR
 PAIRS_PER_BANK = 4
 RUN = 4
 
@@ -82,17 +81,10 @@ def tile_dpfpattention_pb_s_kernel(tc, x, wv, beta, vo, k_phi, W, out):
             nc.sync.dma_start(out=x_sb[:, cols], in_=x_rows[:, cols])
         nc.sync.dma_start(out=beta_rows[0:HEADS, :], in_=beta.flatten_outer_dims())
         nc.sync.dma_start(out=wv_sb[:].rearrange("q (u e) c -> q u (e c)", u=2), in_=wv_rows)
-        def load_vo(group):
+        for group in range(GROUPS):
             heads = slice(group * GROUP_HEADS, (group + 1) * GROUP_HEADS)
             nc.sync.dma_start(out=vo_sb[:, heads, :], in_=vo_rows[:, heads, :])
-
-        load_vo(0)
-        for group in range(GROUPS):
-            if group + 1 < GROUPS:
-                load_vo(group + 1)
-            for pair in range(group * GROUP_PAIRS, (group + 1) * GROUP_PAIRS):
-                heads = slice(pair * PAIR, (pair + 1) * PAIR)
-                nc.sync.dma_start(out=key_sb[:, heads, :], in_=key_rows[:, heads, :])
+            nc.sync.dma_start(out=key_sb[:, heads, :], in_=key_rows[:, heads, :])
         nc.sync.dma_start(out=w_sb[:], in_=w_rows)
 
         x_words = x_sb[:].bitcast(F32)
@@ -182,24 +174,23 @@ def tile_dpfpattention_pb_s_kernel(tc, x, wv, beta, vo, k_phi, W, out):
                 op=ALU.mult,
             )
 
-        def quantise_keys(pair):
-            heads = slice(pair * PAIR, (pair + 1) * PAIR)
-            key_cols = slice(pair * P, (pair + 1) * P)
-            for head in range(pair * PAIR, (pair + 1) * PAIR):
+        def regroup_keys(group):
+            for head in range(group * GROUP_HEADS, (group + 1) * GROUP_HEADS):
                 nc.scalar.copy(
                     out=key_grouped[:, head, :, :].rearrange("p (s i) j -> p s j i", i=RUN),
                     in_=key_sb[:, head, :].rearrange("p (j s i) -> p s j i", j=PACK, i=RUN),
                 )
+
+        def quantise_group(group):
+            heads = slice(group * GROUP_HEADS, (group + 1) * GROUP_HEADS)
+            key_cols = slice(group * GROUP_HEADS * FEATURES, (group + 1) * GROUP_HEADS * FEATURES)
+            dv_cols = slice(group * GROUP_COLS, (group + 1) * GROUP_COLS)
             quantise(
                 nc,
                 key_grouped[:, heads, :, :].rearrange("p h s j -> p (h s j)"),
                 key_codes[:, key_cols],
                 key_scales[:, key_cols],
             )
-
-        def quantise_dv(group):
-            heads = slice(group * GROUP_HEADS, (group + 1) * GROUP_HEADS)
-            dv_cols = slice(group * GROUP_COLS, (group + 1) * GROUP_COLS)
             quantise(
                 nc,
                 dv_grouped[:, heads, :, :].rearrange("p h d j -> p (h d j)"),
@@ -227,11 +218,9 @@ def tile_dpfpattention_pb_s_kernel(tc, x, wv, beta, vo, k_phi, W, out):
             diff_next = subtract(group + 1) if group + 1 < GROUPS else None
             scale(group, diff_now)
             diff_now = diff_next
-            quantise_keys(group * GROUP_PAIRS)
-            quantise_dv(group)
-            for pair in range(group * GROUP_PAIRS + 1, (group + 1) * GROUP_PAIRS):
-                quantise_keys(pair)
-            for pair in range(group * GROUP_PAIRS, (group + 1) * GROUP_PAIRS):
+            regroup_keys(group)
+            quantise_group(group)
+            for pair in range(group * GROUP_HEADS // PAIR, (group + 1) * GROUP_HEADS // PAIR):
                 if pair % PAIRS_PER_BANK == 0:
                     update_bank = others.tile([P, PAIRS_PER_BANK * PAIR * HEAD_DIM], F32, tag="other")
                     update_banks.append(update_bank)

import concourse.mybir as mybir
from concourse.masks import make_identity

F32 = mybir.dt.float32
BF16 = mybir.dt.bfloat16
U32 = mybir.dt.uint32
U8 = mybir.dt.uint8
FP8X4 = mybir.dt.float8_e4m3fn_x4
ALU = mybir.AluOpType

P = 128
PACK = 4
TOKENS = 512
MODEL = 512
HEADS = 16
HEAD_DIM = 32
FEATURES = 64
BANK = 512
PSUM_BANKS = 8

GROUPS = 4
GROUP_HEADS = HEADS // GROUPS
GROUP_COLS = GROUP_HEADS * HEAD_DIM
PAIR = 2
PAIRS = HEADS // PAIR
PAIRS_PER_BANK = 4
RUN = 4

FLOPS = 2 * TOKENS * MODEL * HEADS * HEAD_DIM + 2 * HEADS * FEATURES * TOKENS * HEAD_DIM

assert TOKENS == P * PACK and MODEL == P * PACK and PAIR * FEATURES == P


def quantise(nc, grouped, codes, scales):
    nc.vector.quantize_mx(out=codes.bitcast(FP8X4), scales=scales, in_=grouped)


def tile_dpfpattention_pb_s_kernel(tc, x, wv, beta, vo, k_phi, W, out):
    nc = tc.nc

    x_rows = x.flatten_outer_dims().rearrange("(p j) k -> p (j k)", j=PACK)
    vo_rows = vo.flatten_outer_dims().rearrange("(h p j) d -> p h (j d)", h=HEADS, j=PACK)
    key_rows = k_phi.flatten_outer_dims().rearrange("(h p j) s -> p h (j s)", h=HEADS, j=PACK)
    wv_rows = wv.rearrange("(u q e) c -> q u (e c)", u=2, e=2)
    w_rows = W.flatten_outer_dims().rearrange("(a g s) d -> (g s) a d", a=PAIRS, g=PAIR)
    out_rows = out.flatten_outer_dims().rearrange("(a g s) d -> (g s) a d", a=PAIRS, g=PAIR)

    with tc.tile_pool(name="keep", bufs=1) as keep, tc.tile_pool(
        name="diffs", bufs=2
    ) as diffs, tc.psum_pool(name="values", bufs=GROUPS) as values, tc.psum_pool(
        name="others", bufs=PSUM_BANKS - GROUPS
    ) as others, tc.manual_schedule():
        identity = keep.tile([P, P], F32)
        x_sb = keep.tile([P, PACK * MODEL], BF16)
        x_grouped = keep.tile([P, TOKENS * PACK], BF16, align_bytes=64)
        x_codes = keep.tile([P, TOKENS], U32, align_bytes=64)
        x_scales = keep.tile([P, TOKENS], U8, align_bytes=64)
        wv_sb = keep.tile([P, PACK, HEADS * HEAD_DIM], BF16)
        wv_grouped = keep.tile([P, HEADS * HEAD_DIM, PACK], BF16, align_bytes=64)
        wv_codes = keep.tile([P, HEADS * HEAD_DIM], U32, align_bytes=64)
        wv_scales = keep.tile([P, HEADS * HEAD_DIM], U8, align_bytes=64)
        beta_rows = keep.tile([P, TOKENS], BF16)
        beta_sb = keep.tile([P, HEADS * PACK], BF16)
        vo_sb = keep.tile([P, HEADS, PACK * HEAD_DIM], BF16)
        key_sb = keep.tile([P, HEADS, PACK * FEATURES], BF16)
        key_grouped = keep.tile([P, HEADS, FEATURES, PACK], BF16, align_bytes=64)
        key_codes = keep.tile([P, HEADS * FEATURES], U32, align_bytes=64)
        key_scales = keep.tile([P, HEADS * FEATURES], U8, align_bytes=64)
        dv_grouped = keep.tile([P, HEADS, HEAD_DIM, PACK], BF16, align_bytes=64)
        dv_codes = keep.tile([P, HEADS * HEAD_DIM], U32, align_bytes=64)
        dv_scales = keep.tile([P, HEADS * HEAD_DIM], U8, align_bytes=64)
        w_sb = keep.tile([P, PAIRS, HEAD_DIM], BF16)
        result = keep.tile([P, PAIRS, HEAD_DIM], F32)

        make_identity(nc, identity[:])
        nc.vector.memset(beta_rows[:], 0.0)

        half_row = PACK * MODEL // 2
        for half in range(2):
            cols = slice(half * half_row, (half + 1) * half_row)
            nc.sync.dma_start(out=x_sb[:, cols], in_=x_rows[:, cols])
        nc.sync.dma_start(out=beta_rows[0:HEADS, :], in_=beta.flatten_outer_dims())
        nc.sync.dma_start(out=wv_sb[:].rearrange("q (u e) c -> q u (e c)", u=2), in_=wv_rows)
        for group in range(GROUPS):
            heads = slice(group * GROUP_HEADS, (group + 1) * GROUP_HEADS)
            nc.sync.dma_start(out=vo_sb[:, heads, :], in_=vo_rows[:, heads, :])
            nc.sync.dma_start(out=key_sb[:, heads, :], in_=key_rows[:, heads, :])
        nc.sync.dma_start(out=w_sb[:], in_=w_rows)

        x_words = x_sb[:].bitcast(F32)
        x_grouped_words = x_grouped[:].bitcast(F32)
        def quantise_x(j):
            tokens = slice(j * P, (j + 1) * P)
            quantise(nc, x_grouped[:, j * P * PACK : (j + 1) * P * PACK], x_codes[:, tokens], x_scales[:, tokens])

        for j in range(PACK):
            flipped = others.tile([P, 2 * P], F32, tag="other")
            for u in range(2):
                word = (2 * j + u) * P
                nc.tensor.transpose(flipped[:, u * P : (u + 1) * P], x_words[:, word : word + P], identity[:])
            copy_out = nc.scalar.copy if j % 2 == 0 else nc.vector.tensor_copy
            copy_out(
                out=x_grouped_words[:, j * 2 * P : (j + 1) * 2 * P].rearrange("q (p u) -> q p u", u=2),
                in_=flipped[:].rearrange("q (u p) -> q p u", u=2),
            )
            if j > 0:
                quantise_x(j - 1)

        beta_words = beta_rows[:].bitcast(F32).rearrange("h (p w) -> h w p", w=2)
        beta_flipped = others.tile([P, 2 * P], F32, tag="other")
        for w in range(2):
            nc.tensor.transpose(beta_flipped[:, w * P : (w + 1) * P], beta_words[:, w, :], identity[:])
        nc.scalar.copy(
            out=beta_sb[:].bitcast(F32).rearrange("p (h w) -> p h w", w=2),
            in_=beta_flipped[:].rearrange("p (w h) -> p h w", w=2)[:, 0:HEADS, :],
        )

        def regroup_wv(group):
            cols = slice(group * GROUP_COLS, (group + 1) * GROUP_COLS)
            regroup = nc.vector.tensor_copy if group % 2 == 0 else nc.scalar.copy
            regroup(
                out=wv_grouped[:, cols, :].rearrange("q (c i) t -> q c t i", i=RUN),
                in_=wv_sb[:, :, cols].rearrange("q t (c i) -> q c t i", i=RUN),
            )

        v_banks = []

        def first_matmul(group):
            cols = slice(group * GROUP_COLS, (group + 1) * GROUP_COLS)
            quantise(nc, wv_grouped[:, cols, :].rearrange("q c t -> q (c t)"), wv_codes[:, cols], wv_scales[:, cols])
            v_bank = values.tile([P, BANK], F32)
            v_banks.append(v_bank)
            for j in range(PACK):
                tokens = slice(j * P, (j + 1) * P)
                nc.tensor.matmul_mx(
                    out=v_bank[:, j * GROUP_COLS : (j + 1) * GROUP_COLS],
                    lhsT=x_codes[:, tokens].bitcast(FP8X4),
                    lhsT_scale=x_scales[:, tokens],
                    rhs=wv_codes[:, cols].bitcast(FP8X4),
                    rhs_scale=wv_scales[:, cols],
                    start=True,
                    stop=True,
                )

        regroup_wv(0)
        regroup_wv(1)
        quantise_x(PACK - 1)
        first_matmul(0)
        regroup_wv(2)
        regroup_wv(3)
        for group in range(1, GROUPS):
            first_matmul(group)

        def subtract(group):
            heads = slice(group * GROUP_HEADS, (group + 1) * GROUP_HEADS)
            diff = diffs.tile([P, GROUP_HEADS, HEAD_DIM, PACK], F32)
            nc.vector.tensor_tensor(
                out=diff[:],
                in0=v_banks[group][:].rearrange("p (j h d) -> p h d j", j=PACK, h=GROUP_HEADS),
                in1=vo_sb[:, heads, :].rearrange("p h (j d) -> p h d j", j=PACK),
                op=ALU.subtract,
            )
            return diff

        def scale(group, diff):
            heads = slice(group * GROUP_HEADS, (group + 1) * GROUP_HEADS)
            strengths = beta_sb[:, group * GROUP_HEADS * PACK : (group + 1) * GROUP_HEADS * PACK]
            nc.vector.tensor_tensor(
                out=dv_grouped[:, heads, :, :],
                in0=diff[:],
                in1=strengths.rearrange("p (h j) -> p h j", j=PACK)
                .unsqueeze(2)
                .to_broadcast([P, GROUP_HEADS, HEAD_DIM, PACK]),
                op=ALU.mult,
            )

        def regroup_keys(group):
            for head in range(group * GROUP_HEADS, (group + 1) * GROUP_HEADS):
                nc.scalar.copy(
                    out=key_grouped[:, head, :, :].rearrange("p (s i) j -> p s j i", i=RUN),
                    in_=key_sb[:, head, :].rearrange("p (j s i) -> p s j i", j=PACK, i=RUN),
                )

        def quantise_group(group):
            heads = slice(group * GROUP_HEADS, (group + 1) * GROUP_HEADS)
            key_cols = slice(group * GROUP_HEADS * FEATURES, (group + 1) * GROUP_HEADS * FEATURES)
            dv_cols = slice(group * GROUP_COLS, (group + 1) * GROUP_COLS)
            quantise(
                nc,
                key_grouped[:, heads, :, :].rearrange("p h s j -> p (h s j)"),
                key_codes[:, key_cols],
                key_scales[:, key_cols],
            )
            quantise(
                nc,
                dv_grouped[:, heads, :, :].rearrange("p h d j -> p (h d j)"),
                dv_codes[:, dv_cols],
                dv_scales[:, dv_cols],
            )

        def second_matmul(pair, update_bank):
            key_cols = slice(pair * P, (pair + 1) * P)
            dv_cols = slice(pair * PAIR * HEAD_DIM, (pair + 1) * PAIR * HEAD_DIM)
            place = (pair % PAIRS_PER_BANK) * PAIR * HEAD_DIM
            nc.tensor.matmul_mx(
                out=update_bank[:, place : place + PAIR * HEAD_DIM],
                lhsT=key_codes[:, key_cols].bitcast(FP8X4),
                lhsT_scale=key_scales[:, key_cols],
                rhs=dv_codes[:, dv_cols].bitcast(FP8X4),
                rhs_scale=dv_scales[:, dv_cols],
                start=True,
                stop=True,
            )

        update_banks = []
        diff_now = subtract(0)
        for group in range(GROUPS):
            diff_next = subtract(group + 1) if group + 1 < GROUPS else None
            scale(group, diff_now)
            diff_now = diff_next
            regroup_keys(group)
            quantise_group(group)
            for pair in range(group * GROUP_HEADS // PAIR, (group + 1) * GROUP_HEADS // PAIR):
                if pair % PAIRS_PER_BANK == 0:
                    update_bank = others.tile([P, PAIRS_PER_BANK * PAIR * HEAD_DIM], F32, tag="other")
                    update_banks.append(update_bank)
                second_matmul(pair, update_banks[-1])

        for bank in range(PAIRS // PAIRS_PER_BANK):
            pairs = slice(bank * PAIRS_PER_BANK, (bank + 1) * PAIRS_PER_BANK)
            for g in range(PAIR):
                rows = slice(g * FEATURES, (g + 1) * FEATURES)
                nc.vector.tensor_tensor(
                    out=result[rows, pairs, :],
                    in0=update_banks[bank][rows, :].rearrange(
                        "r (a g d) -> r a g d", a=PAIRS_PER_BANK, g=PAIR
                    )[:, :, g, :],
                    in1=w_sb[rows, pairs, :],
                    op=ALU.add,
                )
            nc.sync.dma_start(out=out_rows[:, pairs, :], in_=result[:, pairs, :])
